import numpy as np
import ml_dtypes


def mxq(x, axis, fmt="e4m3"):
    dtype, down = {"e4m3": (ml_dtypes.float8_e4m3fn, 7), "e5m2": (ml_dtypes.float8_e5m2, 14)}[fmt]
    v = np.moveaxis(np.asarray(x, np.float32).astype(ml_dtypes.bfloat16).astype(np.float64), axis, -1)
    blocks = v.reshape(v.shape[:-1] + (-1, 32))
    amax = np.abs(blocks).max(-1, keepdims=True)
    byte = np.maximum(np.where(amax > 0, np.frexp(amax)[1] - 1 + 127, 0) - down, 1)
    scale = np.exp2(byte - 127.0)
    codes = (blocks / scale).astype(np.float32).astype(dtype).astype(np.float64)
    return np.moveaxis((codes * scale).reshape(v.shape), -1, axis)


WIDE = False


def mx_kscale(k):
    if not WIDE:
        return np.ones(k)
    levels = np.array([10, -10, 5, -5, 0])
    a = np.random.permutation(np.resize(levels, k // 512 * 4)).reshape(k // 512, 4)
    idx = np.arange(k)
    return np.exp2(a[idx // 512, idx % 128 // 32])


BF16 = ml_dtypes.bfloat16


def bf(x):
    return np.asarray(x, np.float32).astype(BF16)


def f64(x):
    return np.asarray(x).astype(np.float64)


E2M1 = np.array([0.0, 0.5, 1.0, 1.5, 2.0, 3.0, 4.0, 6.0, -0.0, -0.5, -1.0, -1.5, -2.0, -3.0, -4.0, -6.0])


def pack_weight(w, fmt):
    k, n = w.shape
    w = f64(bf(w)).reshape(k // 32, 32, n)
    amax = np.abs(w).max(1)
    if fmt == "e4m3":
        byte = np.frexp(amax)[1] - 1 + 127 - 7
    else:
        mant, ex = np.frexp(amax / 6.0)
        byte = np.where(mant > 0.5, ex, ex - 1) + 127
    byte = np.clip(np.where(amax > 0, byte, 1), 1, 254)
    scaled = (w * np.exp2(127.0 - byte)[:, None, :]).reshape(k, n).astype(np.float32)
    by_word = np.ascontiguousarray(scaled.reshape(k // 512, 128, 4, n).transpose(0, 1, 3, 2))
    if fmt == "e4m3":
        words = by_word.astype(ml_dtypes.float8_e4m3fn).view(np.uint8)
    else:
        c = by_word.astype(ml_dtypes.float4_e2m1fn).view(np.uint8) & 0xF
        words = c[..., 0::2] | (c[..., 1::2] << 4)
    return np.ascontiguousarray(words), np.ascontiguousarray(byte.astype(np.uint8).reshape(k // 512, 16, n))


def unpack_weight(words, scales, fmt):
    g, p, n, _ = words.shape
    if fmt == "e4m3":
        vals = np.ascontiguousarray(words).view(ml_dtypes.float8_e4m3fn).astype(np.float64)
    else:
        nib = np.empty((g, p, n, 4), np.uint8)
        nib[..., 0::2] = words & 0xF
        nib[..., 1::2] = words >> 4
        vals = E2M1[nib]
    vals = vals * np.repeat(np.exp2(scales.astype(np.float64) - 127.0), 8, axis=1)[..., None]
    return vals.transpose(0, 1, 3, 2).reshape(g * 512, n)


B, S, DIM, HDIM = 1, 128, 2048, 4096
FMT = "e4m3"


def setup_inputs():
    s = mx_kscale(DIM)
    t = np.exp2(np.round(np.log2(mx_kscale(HDIM)) / 2))
    x = bf(np.random.standard_normal((B, S, DIM)) * s)
    w1 = np.random.standard_normal((HDIM, DIM)) * (1.0 / np.sqrt(DIM)) / s[None, :] * t[:, None]
    w2 = np.random.standard_normal((HDIM, DIM)) * (1.0 / np.sqrt(HDIM)) / (t * t)[:, None]
    W1_words, W1_scales = pack_weight(np.ascontiguousarray(w1.T), FMT)
    W2_words, W2_scales = pack_weight(w2, FMT)
    return {"x": x,
            "W1_words": W1_words, "W1_scales": W1_scales,
            "W2_words": W2_words, "W2_scales": W2_scales}


def reference(x, W1_words, W1_scales, W2_words, W2_scales):
    pre = mxq(f64(x), 2, "e4m3") @ unpack_weight(W1_words, W1_scales, FMT)
    post = np.square(np.maximum(pre, 0.0))
    out = mxq(post, 2, "e4m3") @ unpack_weight(W2_words, W2_scales, FMT)
    return out

@@ -1,0 +1,155 @@
+from contextlib import ExitStack
+
+import concourse.mybir as mybir
+from concourse.masks import make_identity
+
+F32 = mybir.dt.float32
+BF16 = mybir.dt.bfloat16
+I32 = mybir.dt.int32
+U32 = mybir.dt.uint32
+U8 = mybir.dt.uint8
+FP8X4 = mybir.dt.float8_e4m3fn_x4
+ACT = mybir.ActivationFunctionType
+
+P = 128
+DIM = 2048
+HID = 4096
+KP = 512
+NB = 512
+G1 = DIM // KP
+G2 = HID // KP
+FLOPS = 2 * 2 * P * DIM * HID
+
+SCALES_ON_GPSIMD = False
+
+
+def tile_mlp_w_kernel(tc, x, W1_words, W1_scales, W2_words, W2_scales, out):
+    nc = tc.nc
+    with ExitStack() as ctx:
+        keep = ctx.enter_context(tc.tile_pool(name="keep", bufs=1))
+        psum = ctx.enter_context(tc.psum_pool(name="psum", bufs=1))
+        ctx.enter_context(tc.manual_schedule())
+
+        def bank(i, shape, name):
+            return psum.tile(shape, F32, tag="b%d" % i, name=name)
+
+        x2d = x.flatten_outer_dims()
+        out2d = out.flatten_outer_dims()
+
+        ident = keep.tile([P, P], F32, name="ident")
+        x_sb = keep.tile([P, DIM], BF16, name="x_sb")
+        xg = keep.tile([P, DIM], BF16, name="xg", align_bytes=64)
+        xc = keep.tile([P, DIM // 4], U32, name="xc", align_bytes=64)
+        xs = keep.tile([P, DIM // 4], U8, name="xs", align_bytes=64)
+        w1s = keep.tile([P, HID], U8, name="w1s", align_bytes=64)
+        w2s = [keep.tile([P, DIM], U8, name="w2s%d" % h, align_bytes=64) for h in range(2)]
+        w1t = [[keep.tile([P, HID // 2], U32, name="w1t%d_%d" % (h, g), align_bytes=64) for g in range(G1)]
+               for h in range(2)]
+        w2t = [keep.tile([P, DIM], U32, name="w2t%d" % g, align_bytes=64) for g in range(G2 - 1)]
+        w2l = [keep.tile([P, NB], U32, name="w2l%d" % j, align_bytes=64) for j in range(4)]
+        rl = [keep.tile([P, 4, P], F32, name="rl%d" % c) for c in range(G2)]
+        pg = [keep.tile([P, 4, KP], BF16, name="pg%d" % h, align_bytes=64) for h in range(2)]
+        pc = [keep.tile([P, KP], U32, name="pc%d" % h, align_bytes=64) for h in range(2)]
+        ps = [keep.tile([P, KP], U8, name="ps%d" % h, align_bytes=64) for h in range(2)]
+        ob = [keep.tile([P, NB], F32, name="ob%d" % j) for j in range(4)]
+
+        nc.vector.memset(w1s[:].bitcast(I32), 0)
+        for h in range(2):
+            nc.vector.memset(w2s[h][:].bitcast(I32), 0)
+        make_identity(nc, ident[:])
+
+        nc.sync.dma_start(out=x_sb[:], in_=x2d)
+
+        def scale_dma(dst, src):
+            if SCALES_ON_GPSIMD:
+                nc.gpsimd.dma_start(out=dst.bitcast(F32), in_=src.bitcast(F32))
+            else:
+                nc.sync.dma_start(out=dst.bitcast(I32), in_=src.bitcast(I32))
+
+        for q in range(4):
+            scale_dma(w1s[32 * q:32 * q + 16, :], W1_scales[:, 4 * q:4 * q + 4, :])
+        for h in range(2):
+            for q in range(4):
+                scale_dma(w2s[h][32 * q:32 * q + 16, :], W2_scales[4 * h:4 * h + 4, 4 * q:4 * q + 4, :])
+        for h in range(2):
+            for g in range(G1):
+                src = W1_words[g].rearrange("p n t -> p (n t)")[:, 2 * HID * h:2 * HID * (h + 1)]
+                nc.sync.dma_start(out=w1t[h][g][:].bitcast(I32), in_=src.bitcast(I32))
+        for g in range(G2 - 1):
+            src = W2_words[g].rearrange("p n t -> p (n t)")
+            nc.sync.dma_start(out=w2t[g][:].bitcast(I32), in_=src.bitcast(I32))
+        for j in range(4):
+            src = W2_words[G2 - 1].rearrange("p n t -> p (n t)")[:, 4 * NB * j:4 * NB * (j + 1)]
+            nc.sync.dma_start(out=w2l[j][:].bitcast(I32), in_=src.bitcast(I32))
+
+        xw = x_sb[:].bitcast(F32)
+        xgw = xg[:].bitcast(F32)
+        for b in range(2):
+            xt = bank(b, [P, 4, P], "xt%d" % b)
+            for i in range(4):
+                g, u = 2 * b + i // 2, i % 2
+                nc.tensor.transpose(xt[:, i, :], xw[:, 256 * g + u:256 * (g + 1):2], ident[:])
+            dst = xgw[:, 512 * b:512 * (b + 1)].rearrange("p (g r u) -> p g r u", g=2, u=2)
+            src = xt[:].rearrange("p (g u) r -> p g r u", u=2)
+            if b == 0:
+                nc.vector.tensor_copy(out=dst, in_=src)
+            else:
+                nc.scalar.copy(out=dst, in_=src)
+        for b in range(2):
+            nc.vector.quantize_mx(
+                out=xc[:, 256 * b:256 * (b + 1)].bitcast(FP8X4),
+                scales=xs[:, 256 * b:256 * (b + 1)],
+                in_=xg[:, 1024 * b:1024 * (b + 1)],
+            )
+
+        for h in range(2):
+            pre = [bank(4 * h + j, [P, NB], "pre%d" % (4 * h + j)) for j in range(4)]
+            for g in range(G1):
+                for j in range(4):
+                    nc.tensor.matmul_mx(
+                        out=pre[j][:],
+                        lhsT=xc[:, P * g:P * (g + 1)].bitcast(FP8X4),
+                        lhsT_scale=xs[:, P * g:P * (g + 1)],
+                        rhs=w1t[h][g][:, NB * j:NB * (j + 1)].bitcast(FP8X4),
+                        rhs_scale=w1s[4 * g:P, 4 * NB * h + NB * j:4 * NB * h + NB * (j + 1)],
+                        start=(g == 0),
+                        stop=(g == G1 - 1),
+                    )
+            for j in range(4):
+                nc.vector.tensor_scalar_max(
+                    out=rl[4 * h + j][:], in0=pre[j][:].rearrange("m (p t) -> m t p", t=4), scalar1=0.0)
+            for j in range(4):
+                tp = bank(4 * h + j, [P, 4, P], "tp%d" % (4 * h + j))
+                for t in range(4):
+                    nc.tensor.transpose(tp[:, t, :], rl[4 * h + j][:, t, :], ident[:])
+                nc.scalar.activation(
+                    out=pg[h][:, j, :].rearrange("p (r t) -> p r t", t=4),
+                    in_=tp[:].rearrange("p t r -> p r t"),
+                    func=ACT.Square,
+                )
+            nc.vector.quantize_mx(
+                out=pc[h][:].bitcast(FP8X4),
+                scales=ps[h][:],
+                in_=pg[h][:].rearrange("p j c -> p (j c)"),
+            )
+
+        acc = [bank(j, [P, NB], "acc%d" % j) for j in range(4)]
+        for g in range(G2):
+            h, s = g // 4, g % 4
+            for j in range(4):
+                rhs = w2t[g][:, NB * j:NB * (j + 1)] if g < G2 - 1 else w2l[j][:]
+                nc.tensor.matmul_mx(
+                    out=acc[j][:],
+                    lhsT=pc[h][:, P * s:P * (s + 1)].bitcast(FP8X4),
+                    lhsT_scale=ps[h][:, P * s:P * (s + 1)],
+                    rhs=rhs.bitcast(FP8X4),
+                    rhs_scale=w2s[h][4 * s:P, NB * j:NB * (j + 1)],
+                    start=(g == 0),
+                    stop=(g == G2 - 1),
+                )
+        for j in range(4):
+            if j % 2 == 0:
+                nc.vector.tensor_copy(out=ob[j][:], in_=acc[j][:])
+            else:
+                nc.scalar.copy(out=ob[j][:], in_=acc[j][:])
+            nc.sync.dma_start(out=out2d[:, NB * j:NB * (j + 1)], in_=ob[j][:])

@@ -21,6 +21,8 @@ G2 = HID // KP
 FLOPS = 2 * 2 * P * DIM * HID
 
 SCALES_ON_GPSIMD = False
+OUT_W = [512, 512, 512, 256, 128, 128]
+OUT_0 = [0, 512, 1024, 1536, 1792, 1920]
 
 
 def tile_mlp_w_kernel(tc, x, W1_words, W1_scales, W2_words, W2_scales, out):
@@ -46,12 +48,12 @@ def tile_mlp_w_kernel(tc, x, W1_words, W1_scales, W2_words, W2_scales, out):
         w1t = [[keep.tile([P, HID // 2], U32, name="w1t%d_%d" % (h, g), align_bytes=64) for g in range(G1)]
                for h in range(2)]
         w2t = [keep.tile([P, DIM], U32, name="w2t%d" % g, align_bytes=64) for g in range(G2 - 1)]
-        w2l = [keep.tile([P, NB], U32, name="w2l%d" % j, align_bytes=64) for j in range(4)]
+        w2l = [keep.tile([P, w], U32, name="w2l%d" % j, align_bytes=64) for j, w in enumerate(OUT_W)]
         rl = [keep.tile([P, 4, P], F32, name="rl%d" % c) for c in range(G2)]
         pg = [keep.tile([P, 4, KP], BF16, name="pg%d" % h, align_bytes=64) for h in range(2)]
         pc = [keep.tile([P, KP], U32, name="pc%d" % h, align_bytes=64) for h in range(2)]
         ps = [keep.tile([P, KP], U8, name="ps%d" % h, align_bytes=64) for h in range(2)]
-        ob = [keep.tile([P, NB], F32, name="ob%d" % j) for j in range(4)]
+        ob = [keep.tile([P, w], F32, name="ob%d" % j) for j, w in enumerate(OUT_W)]
 
         nc.vector.memset(w1s[:].bitcast(I32), 0)
         for h in range(2):
@@ -78,8 +80,8 @@ def tile_mlp_w_kernel(tc, x, W1_words, W1_scales, W2_words, W2_scales, out):
         for g in range(G2 - 1):
             src = W2_words[g].rearrange("p n t -> p (n t)")
             nc.sync.dma_start(out=w2t[g][:].bitcast(I32), in_=src.bitcast(I32))
-        for j in range(4):
-            src = W2_words[G2 - 1].rearrange("p n t -> p (n t)")[:, 4 * NB * j:4 * NB * (j + 1)]
+        for j, w in enumerate(OUT_W):
+            src = W2_words[G2 - 1].rearrange("p n t -> p (n t)")[:, 4 * OUT_0[j]:4 * (OUT_0[j] + w)]
             nc.sync.dma_start(out=w2l[j][:].bitcast(I32), in_=src.bitcast(I32))
 
         xw = x_sb[:].bitcast(F32)
@@ -133,23 +135,23 @@ def tile_mlp_w_kernel(tc, x, W1_words, W1_scales, W2_words, W2_scales, out):
                 in_=pg[h][:].rearrange("p j c -> p (j c)"),
             )
 
-        acc = [bank(j, [P, NB], "acc%d" % j) for j in range(4)]
+        acc = [bank(j, [P, w], "acc%d" % j) for j, w in enumerate(OUT_W)]
         for g in range(G2):
             h, s = g // 4, g % 4
-            for j in range(4):
-                rhs = w2t[g][:, NB * j:NB * (j + 1)] if g < G2 - 1 else w2l[j][:]
+            for j, w in enumerate(OUT_W):
+                rhs = w2t[g][:, OUT_0[j]:OUT_0[j] + w] if g < G2 - 1 else w2l[j][:]
                 nc.tensor.matmul_mx(
                     out=acc[j][:],
                     lhsT=pc[h][:, P * s:P * (s + 1)].bitcast(FP8X4),
                     lhsT_scale=ps[h][:, P * s:P * (s + 1)],
                     rhs=rhs.bitcast(FP8X4),
-                    rhs_scale=w2s[h][4 * s:P, NB * j:NB * (j + 1)],
+                    rhs_scale=w2s[h][4 * s:P, OUT_0[j]:OUT_0[j] + w],
                     start=(g == 0),
                     stop=(g == G2 - 1),
                 )
-        for j in range(4):
+        for j, w in enumerate(OUT_W):
             if j % 2 == 0:
                 nc.vector.tensor_copy(out=ob[j][:], in_=acc[j][:])
             else:
                 nc.scalar.copy(out=ob[j][:], in_=acc[j][:])
-            nc.sync.dma_start(out=out2d[:, NB * j:NB * (j + 1)], in_=ob[j][:])
+            nc.sync.dma_start(out=out2d[:, OUT_0[j]:OUT_0[j] + w], in_=ob[j][:])

@@ -21,8 +21,6 @@ G2 = HID // KP
 FLOPS = 2 * 2 * P * DIM * HID
 
 SCALES_ON_GPSIMD = False
-OUT_W = [512, 512, 512, 256, 128, 128]
-OUT_0 = [0, 512, 1024, 1536, 1792, 1920]
 
 
 def tile_mlp_w_kernel(tc, x, W1_words, W1_scales, W2_words, W2_scales, out):
@@ -45,15 +43,14 @@ def tile_mlp_w_kernel(tc, x, W1_words, W1_scales, W2_words, W2_scales, out):
         xs = keep.tile([P, DIM // 4], U8, name="xs", align_bytes=64)
         w1s = keep.tile([P, HID], U8, name="w1s", align_bytes=64)
         w2s = [keep.tile([P, DIM], U8, name="w2s%d" % h, align_bytes=64) for h in range(2)]
-        w1t = [[keep.tile([P, HID // 2], U32, name="w1t%d_%d" % (h, g), align_bytes=64) for g in range(G1)]
-               for h in range(2)]
+        w1t = [keep.tile([P, HID], U32, name="w1t%d" % g, align_bytes=64) for g in range(G1)]
         w2t = [keep.tile([P, DIM], U32, name="w2t%d" % g, align_bytes=64) for g in range(G2 - 1)]
-        w2l = [keep.tile([P, w], U32, name="w2l%d" % j, align_bytes=64) for j, w in enumerate(OUT_W)]
+        w2l = [keep.tile([P, NB], U32, name="w2l%d" % j, align_bytes=64) for j in range(4)]
         rl = [keep.tile([P, 4, P], F32, name="rl%d" % c) for c in range(G2)]
         pg = [keep.tile([P, 4, KP], BF16, name="pg%d" % h, align_bytes=64) for h in range(2)]
         pc = [keep.tile([P, KP], U32, name="pc%d" % h, align_bytes=64) for h in range(2)]
         ps = [keep.tile([P, KP], U8, name="ps%d" % h, align_bytes=64) for h in range(2)]
-        ob = [keep.tile([P, w], F32, name="ob%d" % j) for j, w in enumerate(OUT_W)]
+        ob = [keep.tile([P, NB], F32, name="ob%d" % j) for j in range(4)]
 
         nc.vector.memset(w1s[:].bitcast(I32), 0)
         for h in range(2):
@@ -73,15 +70,14 @@ def tile_mlp_w_kernel(tc, x, W1_words, W1_scales, W2_words, W2_scales, out):
         for h in range(2):
             for q in range(4):
                 scale_dma(w2s[h][32 * q:32 * q + 16, :], W2_scales[4 * h:4 * h + 4, 4 * q:4 * q + 4, :])
-        for h in range(2):
-            for g in range(G1):
-                src = W1_words[g].rearrange("p n t -> p (n t)")[:, 2 * HID * h:2 * HID * (h + 1)]
-                nc.sync.dma_start(out=w1t[h][g][:].bitcast(I32), in_=src.bitcast(I32))
+        for g in range(G1):
+            src = W1_words[g].rearrange("p n t -> p (n t)")
+            nc.sync.dma_start(out=w1t[g][:].bitcast(I32), in_=src.bitcast(I32))
         for g in range(G2 - 1):
             src = W2_words[g].rearrange("p n t -> p (n t)")
             nc.sync.dma_start(out=w2t[g][:].bitcast(I32), in_=src.bitcast(I32))
-        for j, w in enumerate(OUT_W):
-            src = W2_words[G2 - 1].rearrange("p n t -> p (n t)")[:, 4 * OUT_0[j]:4 * (OUT_0[j] + w)]
+        for j in range(4):
+            src = W2_words[G2 - 1].rearrange("p n t -> p (n t)")[:, 4 * NB * j:4 * NB * (j + 1)]
             nc.sync.dma_start(out=w2l[j][:].bitcast(I32), in_=src.bitcast(I32))
 
         xw = x_sb[:].bitcast(F32)
@@ -104,54 +100,57 @@ def tile_mlp_w_kernel(tc, x, W1_words, W1_scales, W2_words, W2_scales, out):
                 in_=xg[:, 1024 * b:1024 * (b + 1)],
             )
 
-        for h in range(2):
-            pre = [bank(4 * h + j, [P, NB], "pre%d" % (4 * h + j)) for j in range(4)]
-            for g in range(G1):
-                for j in range(4):
-                    nc.tensor.matmul_mx(
-                        out=pre[j][:],
-                        lhsT=xc[:, P * g:P * (g + 1)].bitcast(FP8X4),
-                        lhsT_scale=xs[:, P * g:P * (g + 1)],
-                        rhs=w1t[h][g][:, NB * j:NB * (j + 1)].bitcast(FP8X4),
-                        rhs_scale=w1s[4 * g:P, 4 * NB * h + NB * j:4 * NB * h + NB * (j + 1)],
-                        start=(g == 0),
-                        stop=(g == G1 - 1),
-                    )
-            for j in range(4):
-                nc.vector.tensor_scalar_max(
-                    out=rl[4 * h + j][:], in0=pre[j][:].rearrange("m (p t) -> m t p", t=4), scalar1=0.0)
-            for j in range(4):
-                tp = bank(4 * h + j, [P, 4, P], "tp%d" % (4 * h + j))
-                for t in range(4):
-                    nc.tensor.transpose(tp[:, t, :], rl[4 * h + j][:, t, :], ident[:])
-                nc.scalar.activation(
-                    out=pg[h][:, j, :].rearrange("p (r t) -> p r t", t=4),
-                    in_=tp[:].rearrange("p t r -> p r t"),
-                    func=ACT.Square,
+        pre = [bank(c, [P, NB], "pre%d" % c) for c in range(G2)]
+        for g in range(G1):
+            for c in range(G2):
+                nc.tensor.matmul_mx(
+                    out=pre[c][:],
+                    lhsT=xc[:, P * g:P * (g + 1)].bitcast(FP8X4),
+                    lhsT_scale=xs[:, P * g:P * (g + 1)],
+                    rhs=w1t[g][:, NB * c:NB * (c + 1)].bitcast(FP8X4),
+                    rhs_scale=w1s[4 * g:P, NB * c:NB * (c + 1)],
+                    start=(g == 0),
+                    stop=(g == G1 - 1),
                 )
+        for c in range(G2):
+            src = pre[c][:].rearrange("m (p t) -> m t p", t=4)
+            if c % 2 == 0:
+                nc.vector.tensor_scalar_max(out=rl[c][:], in0=src, scalar1=0.0)
+            else:
+                nc.scalar.activation(out=rl[c][:], in_=src, func=ACT.Relu)
+        for c in range(G2):
+            tp = bank(c, [P, 4, P], "tp%d" % c)
+            for t in range(4):
+                nc.tensor.transpose(tp[:, t, :], rl[c][:, t, :], ident[:])
+            nc.scalar.activation(
+                out=pg[c // 4][:, c % 4, :].rearrange("p (r t) -> p r t", t=4),
+                in_=tp[:].rearrange("p t r -> p r t"),
+                func=ACT.Square,
+            )
+        for h in range(2):
             nc.vector.quantize_mx(
                 out=pc[h][:].bitcast(FP8X4),
                 scales=ps[h][:],
                 in_=pg[h][:].rearrange("p j c -> p (j c)"),
             )
 
-        acc = [bank(j, [P, w], "acc%d" % j) for j, w in enumerate(OUT_W)]
+        acc = [bank(j, [P, NB], "acc%d" % j) for j in range(4)]
         for g in range(G2):
             h, s = g // 4, g % 4
-            for j, w in enumerate(OUT_W):
-                rhs = w2t[g][:, OUT_0[j]:OUT_0[j] + w] if g < G2 - 1 else w2l[j][:]
+            for j in range(4):
+                rhs = w2t[g][:, NB * j:NB * (j + 1)] if g < G2 - 1 else w2l[j][:]
                 nc.tensor.matmul_mx(
                     out=acc[j][:],
                     lhsT=pc[h][:, P * s:P * (s + 1)].bitcast(FP8X4),
                     lhsT_scale=ps[h][:, P * s:P * (s + 1)],
                     rhs=rhs.bitcast(FP8X4),
-                    rhs_scale=w2s[h][4 * s:P, OUT_0[j]:OUT_0[j] + w],
+                    rhs_scale=w2s[h][4 * s:P, NB * j:NB * (j + 1)],
                     start=(g == 0),
                     stop=(g == G2 - 1),
                 )
-        for j, w in enumerate(OUT_W):
+        for j in range(4):
             if j % 2 == 0:
                 nc.vector.tensor_copy(out=ob[j][:], in_=acc[j][:])
             else:
                 nc.scalar.copy(out=ob[j][:], in_=acc[j][:])
-            nc.sync.dma_start(out=out2d[:, OUT_0[j]:OUT_0[j] + w], in_=ob[j][:])
+            nc.sync.dma_start(out=out2d[:, NB * j:NB * (j + 1)], in_=ob[j][:])

@@ -44,8 +44,7 @@ def tile_mlp_w_kernel(tc, x, W1_words, W1_scales, W2_words, W2_scales, out):
         w1s = keep.tile([P, HID], U8, name="w1s", align_bytes=64)
         w2s = [keep.tile([P, DIM], U8, name="w2s%d" % h, align_bytes=64) for h in range(2)]
         w1t = [keep.tile([P, HID], U32, name="w1t%d" % g, align_bytes=64) for g in range(G1)]
-        w2t = [keep.tile([P, DIM], U32, name="w2t%d" % g, align_bytes=64) for g in range(G2 - 1)]
-        w2l = [keep.tile([P, NB], U32, name="w2l%d" % j, align_bytes=64) for j in range(4)]
+        w2t = [keep.tile([P, DIM], U32, name="w2t%d" % g, align_bytes=64) for g in range(G2)]
         rl = [keep.tile([P, 4, P], F32, name="rl%d" % c) for c in range(G2)]
         pg = [keep.tile([P, 4, KP], BF16, name="pg%d" % h, align_bytes=64) for h in range(2)]
         pc = [keep.tile([P, KP], U32, name="pc%d" % h, align_bytes=64) for h in range(2)]
@@ -73,12 +72,9 @@ def tile_mlp_w_kernel(tc, x, W1_words, W1_scales, W2_words, W2_scales, out):
         for g in range(G1):
             src = W1_words[g].rearrange("p n t -> p (n t)")
             nc.sync.dma_start(out=w1t[g][:].bitcast(I32), in_=src.bitcast(I32))
-        for g in range(G2 - 1):
+        for g in range(G2):
             src = W2_words[g].rearrange("p n t -> p (n t)")
             nc.sync.dma_start(out=w2t[g][:].bitcast(I32), in_=src.bitcast(I32))
-        for j in range(4):
-            src = W2_words[G2 - 1].rearrange("p n t -> p (n t)")[:, 4 * NB * j:4 * NB * (j + 1)]
-            nc.sync.dma_start(out=w2l[j][:].bitcast(I32), in_=src.bitcast(I32))
 
         xw = x_sb[:].bitcast(F32)
         xgw = xg[:].bitcast(F32)
@@ -138,7 +134,7 @@ def tile_mlp_w_kernel(tc, x, W1_words, W1_scales, W2_words, W2_scales, out):
         for g in range(G2):
             h, s = g // 4, g % 4
             for j in range(4):
-                rhs = w2t[g][:, NB * j:NB * (j + 1)] if g < G2 - 1 else w2l[j][:]
+                rhs = w2t[g][:, NB * j:NB * (j + 1)]
                 nc.tensor.matmul_mx(
                     out=acc[j][:],
                     lhsT=pc[h][:, P * s:P * (s + 1)].bitcast(FP8X4),

@@ -21,6 +21,10 @@ G2 = HID // KP
 FLOPS = 2 * 2 * P * DIM * HID
 
 SCALES_ON_GPSIMD = False
+OUT_W = [512, 512, 512, 256, 256]
+OUT_0 = [0, 512, 1024, 1536, 1792]
+WHOLE = 6
+TAIL = [(6, 0, 2), (7, 0, 2), (6, 2, 1), (7, 2, 1), (6, 3, 2), (7, 3, 1), (7, 4, 1)]
 
 
 def tile_mlp_w_kernel(tc, x, W1_words, W1_scales, W2_words, W2_scales, out):
@@ -44,12 +48,14 @@ def tile_mlp_w_kernel(tc, x, W1_words, W1_scales, W2_words, W2_scales, out):
         w1s = keep.tile([P, HID], U8, name="w1s", align_bytes=64)
         w2s = [keep.tile([P, DIM], U8, name="w2s%d" % h, align_bytes=64) for h in range(2)]
         w1t = [keep.tile([P, HID], U32, name="w1t%d" % g, align_bytes=64) for g in range(G1)]
-        w2t = [keep.tile([P, DIM], U32, name="w2t%d" % g, align_bytes=64) for g in range(G2)]
+        w2t = [keep.tile([P, DIM], U32, name="w2t%d" % g, align_bytes=64) for g in range(WHOLE)]
+        w2l = [keep.tile([P, sum(OUT_W[b0:b0 + nb])], U32, name="w2l%d" % i, align_bytes=64)
+               for i, (g, b0, nb) in enumerate(TAIL)]
         rl = [keep.tile([P, 4, P], F32, name="rl%d" % c) for c in range(G2)]
         pg = [keep.tile([P, 4, KP], BF16, name="pg%d" % h, align_bytes=64) for h in range(2)]
         pc = [keep.tile([P, KP], U32, name="pc%d" % h, align_bytes=64) for h in range(2)]
         ps = [keep.tile([P, KP], U8, name="ps%d" % h, align_bytes=64) for h in range(2)]
-        ob = [keep.tile([P, NB], F32, name="ob%d" % j) for j in range(4)]
+        ob = [keep.tile([P, w], F32, name="ob%d" % j) for j, w in enumerate(OUT_W)]
 
         nc.vector.memset(w1s[:].bitcast(I32), 0)
         for h in range(2):
@@ -72,9 +78,13 @@ def tile_mlp_w_kernel(tc, x, W1_words, W1_scales, W2_words, W2_scales, out):
         for g in range(G1):
             src = W1_words[g].rearrange("p n t -> p (n t)")
             nc.sync.dma_start(out=w1t[g][:].bitcast(I32), in_=src.bitcast(I32))
-        for g in range(G2):
+        for g in range(WHOLE):
             src = W2_words[g].rearrange("p n t -> p (n t)")
             nc.sync.dma_start(out=w2t[g][:].bitcast(I32), in_=src.bitcast(I32))
+        for i, (g, b0, nb) in enumerate(TAIL):
+            c0, c1 = OUT_0[b0], OUT_0[b0] + sum(OUT_W[b0:b0 + nb])
+            src = W2_words[g].rearrange("p n t -> p (n t)")[:, 4 * c0:4 * c1]
+            nc.sync.dma_start(out=w2l[i][:].bitcast(I32), in_=src.bitcast(I32))
 
         xw = x_sb[:].bitcast(F32)
         xgw = xg[:].bitcast(F32)
@@ -130,23 +140,29 @@ def tile_mlp_w_kernel(tc, x, W1_words, W1_scales, W2_words, W2_scales, out):
                 in_=pg[h][:].rearrange("p j c -> p (j c)"),
             )
 
-        acc = [bank(j, [P, NB], "acc%d" % j) for j in range(4)]
-        for g in range(G2):
+        acc = [bank(j, [P, w], "acc%d" % j) for j, w in enumerate(OUT_W)]
+
+        def second_pass(g, j, rhs):
             h, s = g // 4, g % 4
-            for j in range(4):
-                rhs = w2t[g][:, NB * j:NB * (j + 1)]
-                nc.tensor.matmul_mx(
-                    out=acc[j][:],
-                    lhsT=pc[h][:, P * s:P * (s + 1)].bitcast(FP8X4),
-                    lhsT_scale=ps[h][:, P * s:P * (s + 1)],
-                    rhs=rhs.bitcast(FP8X4),
-                    rhs_scale=w2s[h][4 * s:P, NB * j:NB * (j + 1)],
-                    start=(g == 0),
-                    stop=(g == G2 - 1),
-                )
-        for j in range(4):
+            nc.tensor.matmul_mx(
+                out=acc[j][:],
+                lhsT=pc[h][:, P * s:P * (s + 1)].bitcast(FP8X4),
+                lhsT_scale=ps[h][:, P * s:P * (s + 1)],
+                rhs=rhs.bitcast(FP8X4),
+                rhs_scale=w2s[h][4 * s:P, OUT_0[j]:OUT_0[j] + OUT_W[j]],
+                start=(g == 0),
+                stop=(g == G2 - 1),
+            )
+
+        for g in range(WHOLE):
+            for j, w in enumerate(OUT_W):
+                second_pass(g, j, w2t[g][:, OUT_0[j]:OUT_0[j] + w])
+        for i, (g, b0, nb) in enumerate(TAIL):
+            for j in range(b0, b0 + nb):
+                second_pass(g, j, w2l[i][:, OUT_0[j] - OUT_0[b0]:OUT_0[j] - OUT_0[b0] + OUT_W[j]])
+        for j, w in enumerate(OUT_W):
             if j % 2 == 0:
                 nc.vector.tensor_copy(out=ob[j][:], in_=acc[j][:])
             else:
                 nc.scalar.copy(out=ob[j][:], in_=acc[j][:])
-            nc.sync.dma_start(out=out2d[:, NB * j:NB * (j + 1)], in_=ob[j][:])
+            nc.sync.dma_start(out=out2d[:, OUT_0[j]:OUT_0[j] + w], in_=ob[j][:])

@@ -20,7 +20,6 @@ G1 = DIM // KP
 G2 = HID // KP
 FLOPS = 2 * 2 * P * DIM * HID
 
-SCALES_ON_GPSIMD = False
 OUT_W = [512, 512, 512, 256, 256]
 OUT_0 = [0, 512, 1024, 1536, 1792]
 WHOLE = 6
@@ -64,17 +63,13 @@ def tile_mlp_w_kernel(tc, x, W1_words, W1_scales, W2_words, W2_scales, out):
 
         nc.sync.dma_start(out=x_sb[:], in_=x2d)
 
-        def scale_dma(dst, src):
-            if SCALES_ON_GPSIMD:
-                nc.gpsimd.dma_start(out=dst.bitcast(F32), in_=src.bitcast(F32))
-            else:
-                nc.sync.dma_start(out=dst.bitcast(I32), in_=src.bitcast(I32))
-
         for q in range(4):
-            scale_dma(w1s[32 * q:32 * q + 16, :], W1_scales[:, 4 * q:4 * q + 4, :])
+            nc.sync.dma_start(out=w1s[32 * q:32 * q + 16, :].bitcast(I32),
+                              in_=W1_scales[:, 4 * q:4 * q + 4, :].bitcast(I32))
         for h in range(2):
             for q in range(4):
-                scale_dma(w2s[h][32 * q:32 * q + 16, :], W2_scales[4 * h:4 * h + 4, 4 * q:4 * q + 4, :])
+                nc.gpsimd.dma_start(out=w2s[h][32 * q:32 * q + 16, :].bitcast(F32),
+                                    in_=W2_scales[4 * h:4 * h + 4, 4 * q:4 * q + 4, :].bitcast(F32))
         for g in range(G1):
             src = W1_words[g].rearrange("p n t -> p (n t)")
             nc.sync.dma_start(out=w1t[g][:].bitcast(I32), in_=src.bitcast(I32))

@@ -46,7 +46,8 @@ def tile_mlp_w_kernel(tc, x, W1_words, W1_scales, W2_words, W2_scales, out):
         xs = keep.tile([P, DIM // 4], U8, name="xs", align_bytes=64)
         w1s = keep.tile([P, HID], U8, name="w1s", align_bytes=64)
         w2s = [keep.tile([P, DIM], U8, name="w2s%d" % h, align_bytes=64) for h in range(2)]
-        w1t = [keep.tile([P, HID], U32, name="w1t%d" % g, align_bytes=64) for g in range(G1)]
+        w1t = [[keep.tile([P, HID // 2], U32, name="w1t%d_%d" % (h, g), align_bytes=64) for g in range(G1)]
+               for h in range(2)]
         w2t = [keep.tile([P, DIM], U32, name="w2t%d" % g, align_bytes=64) for g in range(WHOLE)]
         w2l = [keep.tile([P, sum(OUT_W[b0:b0 + nb])], U32, name="w2l%d" % i, align_bytes=64)
                for i, (g, b0, nb) in enumerate(TAIL)]
@@ -70,9 +71,10 @@ def tile_mlp_w_kernel(tc, x, W1_words, W1_scales, W2_words, W2_scales, out):
             for q in range(4):
                 nc.gpsimd.dma_start(out=w2s[h][32 * q:32 * q + 16, :].bitcast(F32),
                                     in_=W2_scales[4 * h:4 * h + 4, 4 * q:4 * q + 4, :].bitcast(F32))
-        for g in range(G1):
-            src = W1_words[g].rearrange("p n t -> p (n t)")
-            nc.sync.dma_start(out=w1t[g][:].bitcast(I32), in_=src.bitcast(I32))
+        for h in range(2):
+            for g in range(G1):
+                src = W1_words[g].rearrange("p n t -> p (n t)")[:, 2 * HID * h:2 * HID * (h + 1)]
+                nc.sync.dma_start(out=w1t[h][g][:].bitcast(I32), in_=src.bitcast(I32))
         for g in range(WHOLE):
             src = W2_words[g].rearrange("p n t -> p (n t)")
             nc.sync.dma_start(out=w2t[g][:].bitcast(I32), in_=src.bitcast(I32))
@@ -101,34 +103,36 @@ def tile_mlp_w_kernel(tc, x, W1_words, W1_scales, W2_words, W2_scales, out):
                 in_=xg[:, 1024 * b:1024 * (b + 1)],
             )
 
-        pre = [bank(c, [P, NB], "pre%d" % c) for c in range(G2)]
-        for g in range(G1):
-            for c in range(G2):
-                nc.tensor.matmul_mx(
-                    out=pre[c][:],
-                    lhsT=xc[:, P * g:P * (g + 1)].bitcast(FP8X4),
-                    lhsT_scale=xs[:, P * g:P * (g + 1)],
-                    rhs=w1t[g][:, NB * c:NB * (c + 1)].bitcast(FP8X4),
-                    rhs_scale=w1s[4 * g:P, NB * c:NB * (c + 1)],
-                    start=(g == 0),
-                    stop=(g == G1 - 1),
-                )
-        for c in range(G2):
-            src = pre[c][:].rearrange("m (p t) -> m t p", t=4)
-            if c % 2 == 0:
-                nc.vector.tensor_scalar_max(out=rl[c][:], in0=src, scalar1=0.0)
-            else:
-                nc.scalar.activation(out=rl[c][:], in_=src, func=ACT.Relu)
-        for c in range(G2):
-            tp = bank(c, [P, 4, P], "tp%d" % c)
-            for t in range(4):
-                nc.tensor.transpose(tp[:, t, :], rl[c][:, t, :], ident[:])
-            nc.scalar.activation(
-                out=pg[c // 4][:, c % 4, :].rearrange("p (r t) -> p r t", t=4),
-                in_=tp[:].rearrange("p t r -> p r t"),
-                func=ACT.Square,
-            )
         for h in range(2):
+            cs = range(4 * h, 4 * h + 4)
+            pre = {c: bank(c, [P, NB], "pre%d" % c) for c in cs}
+            for g in range(G1):
+                for c in cs:
+                    n0 = NB * (c - 4 * h)
+                    nc.tensor.matmul_mx(
+                        out=pre[c][:],
+                        lhsT=xc[:, P * g:P * (g + 1)].bitcast(FP8X4),
+                        lhsT_scale=xs[:, P * g:P * (g + 1)],
+                        rhs=w1t[h][g][:, n0:n0 + NB].bitcast(FP8X4),
+                        rhs_scale=w1s[4 * g:P, NB * c:NB * (c + 1)],
+                        start=(g == 0),
+                        stop=(g == G1 - 1),
+                    )
+            for c in cs:
+                src = pre[c][:].rearrange("m (p t) -> m t p", t=4)
+                if c % 2 == 0:
+                    nc.vector.tensor_scalar_max(out=rl[c][:], in0=src, scalar1=0.0)
+                else:
+                    nc.scalar.activation(out=rl[c][:], in_=src, func=ACT.Relu)
+            for c in cs:
+                tp = bank(c, [P, 4, P], "tp%d" % c)
+                for t in range(4):
+                    nc.tensor.transpose(tp[:, t, :], rl[c][:, t, :], ident[:])
+                nc.scalar.activation(
+                    out=pg[h][:, c % 4, :].rearrange("p (r t) -> p r t", t=4),
+                    in_=tp[:].rearrange("p t r -> p r t"),
+                    func=ACT.Square,
+                )
             nc.vector.quantize_mx(
                 out=pc[h][:].bitcast(FP8X4),
                 scales=ps[h][:],

@@ -64,9 +64,6 @@ def tile_mlp_w_kernel(tc, x, W1_words, W1_scales, W2_words, W2_scales, out):
 
         nc.sync.dma_start(out=x_sb[:], in_=x2d)
 
-        for q in range(4):
-            nc.sync.dma_start(out=w1s[32 * q:32 * q + 16, :].bitcast(I32),
-                              in_=W1_scales[:, 4 * q:4 * q + 4, :].bitcast(I32))
         for h in range(2):
             for q in range(4):
                 nc.gpsimd.dma_start(out=w2s[h][32 * q:32 * q + 16, :].bitcast(F32),
@@ -75,6 +72,10 @@ def tile_mlp_w_kernel(tc, x, W1_words, W1_scales, W2_words, W2_scales, out):
             for g in range(G1):
                 src = W1_words[g].rearrange("p n t -> p (n t)")[:, 2 * HID * h:2 * HID * (h + 1)]
                 nc.sync.dma_start(out=w1t[h][g][:].bitcast(I32), in_=src.bitcast(I32))
+                if h == 0 and g == 0:
+                    for q in range(4):
+                        nc.sync.dma_start(out=w1s[32 * q:32 * q + 16, :].bitcast(I32),
+                                          in_=W1_scales[:, 4 * q:4 * q + 4, :].bitcast(I32))
         for g in range(WHOLE):
             src = W2_words[g].rearrange("p n t -> p (n t)")
             nc.sync.dma_start(out=w2t[g][:].bitcast(I32), in_=src.bitcast(I32))

from contextlib import ExitStack

import concourse.mybir as mybir
from concourse.masks import make_identity

F32 = mybir.dt.float32
BF16 = mybir.dt.bfloat16
I32 = mybir.dt.int32
U32 = mybir.dt.uint32
U8 = mybir.dt.uint8
FP8X4 = mybir.dt.float8_e4m3fn_x4
ACT = mybir.ActivationFunctionType

P = 128
DIM = 2048
HID = 4096
KP = 512
NB = 512
G1 = DIM // KP
G2 = HID // KP
FLOPS = 2 * 2 * P * DIM * HID

OUT_W = [512, 512, 512, 256, 256]
OUT_0 = [0, 512, 1024, 1536, 1792]
WHOLE = 6
TAIL = [(6, 0, 2), (7, 0, 2), (6, 2, 1), (7, 2, 1), (6, 3, 2), (7, 3, 1), (7, 4, 1)]


def tile_mlp_w_kernel(tc, x, W1_words, W1_scales, W2_words, W2_scales, out):
    nc = tc.nc
    with ExitStack() as ctx:
        keep = ctx.enter_context(tc.tile_pool(name="keep", bufs=1))
        psum = ctx.enter_context(tc.psum_pool(name="psum", bufs=1))
        ctx.enter_context(tc.manual_schedule())

        def bank(i, shape, name):
            return psum.tile(shape, F32, tag="b%d" % i, name=name)

        x2d = x.flatten_outer_dims()
        out2d = out.flatten_outer_dims()

        ident = keep.tile([P, P], F32, name="ident")
        x_sb = keep.tile([P, DIM], BF16, name="x_sb")
        xg = keep.tile([P, DIM], BF16, name="xg", align_bytes=64)
        xc = keep.tile([P, DIM // 4], U32, name="xc", align_bytes=64)
        xs = keep.tile([P, DIM // 4], U8, name="xs", align_bytes=64)
        w1s = keep.tile([P, HID], U8, name="w1s", align_bytes=64)
        w2s = [keep.tile([P, DIM], U8, name="w2s%d" % h, align_bytes=64) for h in range(2)]
        w1t = [[keep.tile([P, HID // 2], U32, name="w1t%d_%d" % (h, g), align_bytes=64) for g in range(G1)]
               for h in range(2)]
        w2t = [keep.tile([P, DIM], U32, name="w2t%d" % g, align_bytes=64) for g in range(WHOLE)]
        w2l = [keep.tile([P, sum(OUT_W[b0:b0 + nb])], U32, name="w2l%d" % i, align_bytes=64)
               for i, (g, b0, nb) in enumerate(TAIL)]
        rl = [keep.tile([P, 4, P], F32, name="rl%d" % c) for c in range(G2)]
        pg = [keep.tile([P, 4, KP], BF16, name="pg%d" % h, align_bytes=64) for h in range(2)]
        pc = [keep.tile([P, KP], U32, name="pc%d" % h, align_bytes=64) for h in range(2)]
        ps = [keep.tile([P, KP], U8, name="ps%d" % h, align_bytes=64) for h in range(2)]
        ob = [keep.tile([P, w], F32, name="ob%d" % j) for j, w in enumerate(OUT_W)]

        nc.vector.memset(w1s[:].bitcast(I32), 0)
        for h in range(2):
            nc.vector.memset(w2s[h][:].bitcast(I32), 0)
        make_identity(nc, ident[:])

        nc.sync.dma_start(out=x_sb[:], in_=x2d)

        for h in range(2):
            for q in range(4):
                nc.gpsimd.dma_start(out=w2s[h][32 * q:32 * q + 16, :].bitcast(F32),
                                    in_=W2_scales[4 * h:4 * h + 4, 4 * q:4 * q + 4, :].bitcast(F32))
        for h in range(2):
            for g in range(G1):
                src = W1_words[g].rearrange("p n t -> p (n t)")[:, 2 * HID * h:2 * HID * (h + 1)]
                nc.sync.dma_start(out=w1t[h][g][:].bitcast(I32), in_=src.bitcast(I32))
                if h == 0 and g == 0:
                    for q in range(4):
                        nc.sync.dma_start(out=w1s[32 * q:32 * q + 16, :].bitcast(I32),
                                          in_=W1_scales[:, 4 * q:4 * q + 4, :].bitcast(I32))
        for g in range(WHOLE):
            src = W2_words[g].rearrange("p n t -> p (n t)")
            nc.sync.dma_start(out=w2t[g][:].bitcast(I32), in_=src.bitcast(I32))
        for i, (g, b0, nb) in enumerate(TAIL):
            c0, c1 = OUT_0[b0], OUT_0[b0] + sum(OUT_W[b0:b0 + nb])
            src = W2_words[g].rearrange("p n t -> p (n t)")[:, 4 * c0:4 * c1]
            nc.sync.dma_start(out=w2l[i][:].bitcast(I32), in_=src.bitcast(I32))

        xw = x_sb[:].bitcast(F32)
        xgw = xg[:].bitcast(F32)
        for b in range(2):
            xt = bank(b, [P, 4, P], "xt%d" % b)
            for i in range(4):
                g, u = 2 * b + i // 2, i % 2
                nc.tensor.transpose(xt[:, i, :], xw[:, 256 * g + u:256 * (g + 1):2], ident[:])
            dst = xgw[:, 512 * b:512 * (b + 1)].rearrange("p (g r u) -> p g r u", g=2, u=2)
            src = xt[:].rearrange("p (g u) r -> p g r u", u=2)
            if b == 0:
                nc.vector.tensor_copy(out=dst, in_=src)
            else:
                nc.scalar.copy(out=dst, in_=src)
        for b in range(2):
            nc.vector.quantize_mx(
                out=xc[:, 256 * b:256 * (b + 1)].bitcast(FP8X4),
                scales=xs[:, 256 * b:256 * (b + 1)],
                in_=xg[:, 1024 * b:1024 * (b + 1)],
            )

        for h in range(2):
            cs = range(4 * h, 4 * h + 4)
            pre = {c: bank(c, [P, NB], "pre%d" % c) for c in cs}
            for g in range(G1):
                for c in cs:
                    n0 = NB * (c - 4 * h)
                    nc.tensor.matmul_mx(
                        out=pre[c][:],
                        lhsT=xc[:, P * g:P * (g + 1)].bitcast(FP8X4),
                        lhsT_scale=xs[:, P * g:P * (g + 1)],
                        rhs=w1t[h][g][:, n0:n0 + NB].bitcast(FP8X4),
                        rhs_scale=w1s[4 * g:P, NB * c:NB * (c + 1)],
                        start=(g == 0),
                        stop=(g == G1 - 1),
                    )
            for c in cs:
                src = pre[c][:].rearrange("m (p t) -> m t p", t=4)
                if c % 2 == 0:
                    nc.vector.tensor_scalar_max(out=rl[c][:], in0=src, scalar1=0.0)
                else:
                    nc.scalar.activation(out=rl[c][:], in_=src, func=ACT.Relu)
            for c in cs:
                tp = bank(c, [P, 4, P], "tp%d" % c)
                for t in range(4):
                    nc.tensor.transpose(tp[:, t, :], rl[c][:, t, :], ident[:])
                nc.scalar.activation(
                    out=pg[h][:, c % 4, :].rearrange("p (r t) -> p r t", t=4),
                    in_=tp[:].rearrange("p t r -> p r t"),
                    func=ACT.Square,
                )
            nc.vector.quantize_mx(
                out=pc[h][:].bitcast(FP8X4),
                scales=ps[h][:],
                in_=pg[h][:].rearrange("p j c -> p (j c)"),
            )

        acc = [bank(j, [P, w], "acc%d" % j) for j, w in enumerate(OUT_W)]

        def second_pass(g, j, rhs):
            h, s = g // 4, g % 4
            nc.tensor.matmul_mx(
                out=acc[j][:],
                lhsT=pc[h][:, P * s:P * (s + 1)].bitcast(FP8X4),
                lhsT_scale=ps[h][:, P * s:P * (s + 1)],
                rhs=rhs.bitcast(FP8X4),
                rhs_scale=w2s[h][4 * s:P, OUT_0[j]:OUT_0[j] + OUT_W[j]],
                start=(g == 0),
                stop=(g == G2 - 1),
            )

        for g in range(WHOLE):
            for j, w in enumerate(OUT_W):
                second_pass(g, j, w2t[g][:, OUT_0[j]:OUT_0[j] + w])
        for i, (g, b0, nb) in enumerate(TAIL):
            for j in range(b0, b0 + nb):
                second_pass(g, j, w2l[i][:, OUT_0[j] - OUT_0[b0]:OUT_0[j] - OUT_0[b0] + OUT_W[j]])
        for j, w in enumerate(OUT_W):
            if j % 2 == 0:
                nc.vector.tensor_copy(out=ob[j][:], in_=acc[j][:])
            else:
                nc.scalar.copy(out=ob[j][:], in_=acc[j][:])
            nc.sync.dma_start(out=out2d[:, OUT_0[j]:OUT_0[j] + w], in_=ob[j][:])
